import numpy as np
import ml_dtypes


def mxq(x, axis, fmt="e4m3"):
    dtype, down = {"e4m3": (ml_dtypes.float8_e4m3fn, 7), "e5m2": (ml_dtypes.float8_e5m2, 14)}[fmt]
    v = np.moveaxis(np.asarray(x, np.float32).astype(ml_dtypes.bfloat16).astype(np.float64), axis, -1)
    blocks = v.reshape(v.shape[:-1] + (-1, 32))
    amax = np.abs(blocks).max(-1, keepdims=True)
    byte = np.maximum(np.where(amax > 0, np.frexp(amax)[1] - 1 + 127, 0) - down, 1)
    scale = np.exp2(byte - 127.0)
    codes = (blocks / scale).astype(np.float32).astype(dtype).astype(np.float64)
    return np.moveaxis((codes * scale).reshape(v.shape), -1, axis)


WIDE = False


def mx_kscale(k):
    if not WIDE:
        return np.ones(k)
    levels = np.array([10, -10, 5, -5, 0])
    a = np.random.permutation(np.resize(levels, k // 512 * 4)).reshape(k // 512, 4)
    idx = np.arange(k)
    return np.exp2(a[idx // 512, idx % 128 // 32])


BF16 = ml_dtypes.bfloat16


def bf(x):
    return np.asarray(x, np.float32).astype(BF16)


def f64(x):
    return np.asarray(x).astype(np.float64)


B, F, N = 16, 512, 512


def setup_inputs():
    t = mx_kscale(N)
    u = t / t.min()
    amp = np.random.uniform(0.5, 1.5, (B, 1, N))
    emb = np.random.uniform(1e-3, 1.0, (B, F, N)) * amp * np.sqrt(5.0 / F)
    mom = np.random.uniform(0.2, 1.0, (B, N))
    alpha_p = bf(0.6 + 0.3 * np.random.uniform(size=(1, 1)))
    beta_p = bf(1.15 + 0.2 * np.random.uniform(size=(1, 1, 1)))
    a = float(f64(alpha_p)[0, 0])
    emb = emb * u[None, None, :]
    emb[:, 4, :] = mom * u[None, :] ** (-1.0 / a)
    return {"emb": bf(emb), "alpha_p": alpha_p, "beta_p": beta_p}


def reference(emb, alpha_p, beta_p):
    e = f64(emb)
    sq_norms = np.sum(e * e, axis=1)
    eq = mxq(e, 1, "e4m3")
    gram = eq.transpose(0, 2, 1) @ eq
    sqdist = sq_norms[:, :, None] + sq_norms[:, None, :] - 2.0 * gram
    momentum = e[:, 4, :]
    alpha = f64(alpha_p)[0, 0]
    pow_momenta = np.exp(2.0 * alpha * np.log(momentum))
    min_momenta = np.minimum(pow_momenta[:, :, None], pow_momenta[:, None, :])
    d_ij = sqdist * min_momenta
    beta_sq = f64(beta_p)[0, 0, 0] ** 2
    return np.exp(-beta_sq * d_ij)

@@ -1,0 +1,194 @@
+from contextlib import ExitStack
+
+import concourse.mybir as mybir
+from concourse.masks import make_identity
+
+F32 = mybir.dt.float32
+BF16 = mybir.dt.bfloat16
+U32 = mybir.dt.uint32
+U8 = mybir.dt.uint8
+FP8X4 = mybir.dt.float8_e4m3fn_x4
+ACT = mybir.ActivationFunctionType
+ALU = mybir.AluOpType
+
+B, F, N = 16, 512, 512
+P = 128
+PACK = 4
+ROWS = N // P
+MOMENTUM = 4
+MOVING = (512, 512, 256, 128)
+
+FLOPS = 2 * B * N * N * F
+
+
+def tile_qcdawareold_t_kernel(tc, emb, alpha_p, beta_p, out):
+    nc = tc.nc
+    with ExitStack() as ctx:
+        const = ctx.enter_context(tc.tile_pool(name="const", bufs=1))
+        raw_pool = ctx.enter_context(tc.tile_pool(name="raw", bufs=B))
+        mx_pool = ctx.enter_context(tc.tile_pool(name="mx", bufs=3))
+        stat_pool = ctx.enter_context(tc.tile_pool(name="stat", bufs=3))
+        square_pool = ctx.enter_context(tc.tile_pool(name="square", bufs=4))
+        diff_pool = ctx.enter_context(tc.tile_pool(name="diff", bufs=4))
+        expo_pool = ctx.enter_context(tc.tile_pool(name="expo", bufs=3))
+        out_pool = ctx.enter_context(tc.tile_pool(name="outp", bufs=3))
+        psum_feat = ctx.enter_context(tc.psum_pool(name="psum_feat", bufs=2))
+        psum_gram = ctx.enter_context(tc.psum_pool(name="psum_gram", bufs=2))
+        psum_rows = ctx.enter_context(tc.psum_pool(name="psum_rows", bufs=1))
+        psum_mirror = ctx.enter_context(tc.psum_pool(name="psum_mirror", bufs=2))
+
+        alpha_bf = const.tile([P, 1], BF16)
+        nc.scalar.dma_start(out=alpha_bf[:], in_=alpha_p.rearrange("a b -> (a b)").partition_broadcast(P))
+        beta_bf = const.tile([P, 1], BF16)
+        nc.scalar.dma_start(out=beta_bf[:], in_=beta_p.rearrange("a b c -> (a b c)").partition_broadcast(P))
+        mom_rows = const.tile([P, N], BF16)
+        nc.vector.memset(mom_rows[:], 0.0)
+        nc.scalar.dma_start(out=mom_rows[0:B, :], in_=emb[:, MOMENTUM, :])
+
+        raw = []
+        for b in range(B):
+            e_raw = raw_pool.tile([P, PACK, N], BF16)
+            nc.sync.dma_start(out=e_raw[:], in_=emb[b].rearrange("(p t) n -> p t n", t=PACK))
+            raw.append(e_raw)
+
+        ident_bf = const.tile([P, P], BF16)
+        make_identity(nc, ident_bf[:])
+        ident_f32 = const.tile([P, P], F32)
+        make_identity(nc, ident_f32[:])
+
+        two_alpha = const.tile([P, 1], F32)
+        nc.vector.tensor_scalar_mul(out=two_alpha[:], in0=alpha_bf[:], scalar1=2.0)
+        two_beta_sq = const.tile([P, 1], F32)
+        nc.vector.scalar_tensor_tensor(
+            out=two_beta_sq[:], in0=beta_bf[:], scalar=2.0, in1=beta_bf[:], op0=ALU.mult, op1=ALU.mult
+        )
+        mom_cols = psum_feat.tile([P, ROWS, P], BF16, tag="feat")
+        for r in range(ROWS):
+            nc.tensor.transpose(mom_cols[:, r, :], mom_rows[:, P * r : P * (r + 1)], ident_bf[:])
+        log_mom = const.tile([P, ROWS, B], F32)
+        nc.scalar.activation(out=log_mom[:], in_=mom_cols[:, :, 0:B], func=ACT.Ln)
+        pow_mom = const.tile([P, ROWS, B], F32)
+        nc.scalar.activation(out=pow_mom[:], in_=log_mom[:], func=ACT.Exp, scale=two_alpha[:])
+        q_col = const.tile([P, ROWS, B], F32)
+        nc.vector.tensor_scalar_mul(out=q_col[:], in0=pow_mom[:], scalar1=two_beta_sq[:])
+
+        h_cols = {}
+        h_rows = {}
+        q_rows = {}
+        grouped_tiles = {}
+        code_tiles = {}
+        scale_tiles = {}
+
+        def half_norms(b):
+            n_col = stat_pool.tile([P, ROWS], F32)
+            for r in range(ROWS):
+                feat = psum_feat.tile([P, PACK, P], BF16, tag="feat")
+                for t in range(PACK):
+                    nc.tensor.transpose(feat[:, t, :], raw[b][:, t, P * r : P * (r + 1)], ident_bf[:])
+                squares = square_pool.tile([P, PACK, P], BF16)
+                nc.scalar.activation(out=squares[:], in_=feat[:], func=ACT.Square, accum_out=n_col[:, r : r + 1])
+            h_col = stat_pool.tile([P, ROWS], F32)
+            nc.scalar.mul(out=h_col[:], in_=n_col[:], mul=0.5)
+            h_cols[b] = h_col
+
+        def spread(row, column_of):
+            for r in range(ROWS):
+                nc.tensor.transpose(row[:, P * r : P * (r + 1)], column_of(r).to_broadcast([P, P]), ident_f32[:])
+
+        def rows_of(b):
+            h_row_psum = psum_rows.tile([P, N], F32)
+            spread(h_row_psum, lambda r: h_cols[b][:, r : r + 1])
+            h_row = stat_pool.tile([P, N], F32)
+            nc.vector.tensor_copy(out=h_row[:], in_=h_row_psum[:])
+            h_rows[b] = h_row
+            q_row = psum_rows.tile([P, N], F32)
+            spread(q_row, lambda r: q_col[:, r, b : b + 1])
+            q_rows[b] = q_row
+
+        def regroup(b):
+            grouped = mx_pool.tile([P, N, PACK], BF16, align_bytes=64)
+            nc.vector.tensor_copy(
+                out=grouped[:].rearrange("p (c i) t -> p c t i", i=4),
+                in_=raw[b][:].rearrange("p t (c i) -> p c t i", i=4),
+            )
+            grouped_tiles[b] = grouped
+
+        def quantise(b):
+            codes = mx_pool.tile([P, N], U32, align_bytes=64)
+            scales = mx_pool.tile([P, N], U8, align_bytes=64)
+            nc.vector.quantize_mx(
+                out=codes[:].bitcast(FP8X4),
+                scales=scales[:],
+                in_=grouped_tiles[b][:].rearrange("p n t -> p (n t)"),
+            )
+            code_tiles[b] = codes
+            scale_tiles[b] = scales
+
+        def weights(b):
+            codes, scales = code_tiles[b], scale_tiles[b]
+            expo = expo_pool.tile([P, ROWS, N], F32)
+            result = out_pool.tile([P, ROWS, N], F32)
+            diffs = {}
+
+            def difference(r):
+                first = N - MOVING[r]
+                gram = psum_gram.tile([P, N], F32)
+                nc.tensor.matmul_mx(
+                    out=gram[:, first:N],
+                    lhsT=codes[:, P * r : P * (r + 1)].bitcast(FP8X4),
+                    lhsT_scale=scales[:, P * r : P * (r + 1)],
+                    rhs=codes[:, first:N].bitcast(FP8X4),
+                    rhs_scale=scales[:, first:N],
+                    start=True,
+                    stop=True,
+                )
+                diff = diff_pool.tile([P, N], F32)
+                nc.vector.scalar_tensor_tensor(
+                    out=diff[:, P * r : N],
+                    in0=gram[:, P * r : N],
+                    scalar=h_cols[b][:, r : r + 1],
+                    in1=h_rows[b][:, P * r : N],
+                    op0=ALU.subtract,
+                    op1=ALU.subtract,
+                )
+                diffs[r] = diff
+
+            def exponent(r):
+                nc.vector.scalar_tensor_tensor(
+                    out=expo[:, r, P * r : N],
+                    in0=q_rows[b][:, P * r : N],
+                    scalar=q_col[:, r, b : b + 1],
+                    in1=diffs[r][:, P * r : N],
+                    op0=ALU.min,
+                    op1=ALU.mult,
+                )
+                nc.scalar.activation(out=result[:, r, P * r : N], in_=expo[:, r, P * r : N], func=ACT.Exp)
+
+            for r in range(ROWS + 1):
+                if r < ROWS:
+                    difference(r)
+                if r > 0:
+                    exponent(r - 1)
+
+            for r in range(1, ROWS):
+                mirror = psum_mirror.tile([P, N], F32)
+                for c in range(r):
+                    nc.tensor.transpose(mirror[:, P * c : P * (c + 1)], expo[:, c, P * r : P * (r + 1)], ident_f32[:])
+                nc.scalar.activation(out=result[:, r, 0 : P * r], in_=mirror[:, 0 : P * r], func=ACT.Exp)
+
+            nc.sync.dma_start(out=out[b].rearrange("(r p) j -> p r j", p=P), in_=result[:])
+
+        half_norms(0)
+        rows_of(0)
+        regroup(0)
+        regroup(1)
+        quantise(0)
+        for b in range(B):
+            if b + 1 < B:
+                half_norms(b + 1)
+            weights(b)
+            if b + 2 < B:
+                regroup(b + 2)
+            if b + 1 < B:
+                quantise(b + 1)
+                rows_of(b + 1)

@@ -1,3 +1,4 @@
+import math
 from contextlib import ExitStack
 
 import concourse.mybir as mybir
@@ -16,7 +17,6 @@ P = 128
 PACK = 4
 ROWS = N // P
 MOMENTUM = 4
-MOVING = (512, 512, 256, 128)
 
 FLOPS = 2 * B * N * N * F
 
@@ -24,26 +24,27 @@ FLOPS = 2 * B * N * N * F
 def tile_qcdawareold_t_kernel(tc, emb, alpha_p, beta_p, out):
     nc = tc.nc
     with ExitStack() as ctx:
+        ctx.enter_context(tc.manual_schedule())
         const = ctx.enter_context(tc.tile_pool(name="const", bufs=1))
         raw_pool = ctx.enter_context(tc.tile_pool(name="raw", bufs=B))
+        grouped_pool = ctx.enter_context(tc.tile_pool(name="grouped", bufs=1))
         mx_pool = ctx.enter_context(tc.tile_pool(name="mx", bufs=3))
-        stat_pool = ctx.enter_context(tc.tile_pool(name="stat", bufs=3))
+        stat_pool = ctx.enter_context(tc.tile_pool(name="stat", bufs=4))
         square_pool = ctx.enter_context(tc.tile_pool(name="square", bufs=4))
         diff_pool = ctx.enter_context(tc.tile_pool(name="diff", bufs=4))
-        expo_pool = ctx.enter_context(tc.tile_pool(name="expo", bufs=3))
+        expo_pool = ctx.enter_context(tc.tile_pool(name="expo", bufs=2))
         out_pool = ctx.enter_context(tc.tile_pool(name="outp", bufs=3))
-        psum_feat = ctx.enter_context(tc.psum_pool(name="psum_feat", bufs=2))
-        psum_gram = ctx.enter_context(tc.psum_pool(name="psum_gram", bufs=2))
-        psum_rows = ctx.enter_context(tc.psum_pool(name="psum_rows", bufs=1))
-        psum_mirror = ctx.enter_context(tc.psum_pool(name="psum_mirror", bufs=2))
+        psum_gram = ctx.enter_context(tc.psum_pool(name="psum_gram", bufs=1))
+        psum_q = ctx.enter_context(tc.psum_pool(name="psum_q", bufs=1))
+        psum_stage = ctx.enter_context(tc.psum_pool(name="psum_stage", bufs=4))
 
+        mom_rows = const.tile([P, N], BF16)
+        nc.vector.memset(mom_rows[:], 0.0)
+        nc.scalar.dma_start(out=mom_rows[0:B, :], in_=emb[:, MOMENTUM, :])
         alpha_bf = const.tile([P, 1], BF16)
         nc.scalar.dma_start(out=alpha_bf[:], in_=alpha_p.rearrange("a b -> (a b)").partition_broadcast(P))
         beta_bf = const.tile([P, 1], BF16)
         nc.scalar.dma_start(out=beta_bf[:], in_=beta_p.rearrange("a b c -> (a b c)").partition_broadcast(P))
-        mom_rows = const.tile([P, N], BF16)
-        nc.vector.memset(mom_rows[:], 0.0)
-        nc.scalar.dma_start(out=mom_rows[0:B, :], in_=emb[:, MOMENTUM, :])
 
         raw = []
         for b in range(B):
@@ -62,7 +63,7 @@ def tile_qcdawareold_t_kernel(tc, emb, alpha_p, beta_p, out):
         nc.vector.scalar_tensor_tensor(
             out=two_beta_sq[:], in0=beta_bf[:], scalar=2.0, in1=beta_bf[:], op0=ALU.mult, op1=ALU.mult
         )
-        mom_cols = psum_feat.tile([P, ROWS, P], BF16, tag="feat")
+        mom_cols = psum_stage.tile([P, ROWS, P], BF16, tag="stage")
         for r in range(ROWS):
             nc.tensor.transpose(mom_cols[:, r, :], mom_rows[:, P * r : P * (r + 1)], ident_bf[:])
         log_mom = const.tile([P, ROWS, B], F32)
@@ -73,43 +74,57 @@ def tile_qcdawareold_t_kernel(tc, emb, alpha_p, beta_p, out):
         nc.vector.tensor_scalar_mul(out=q_col[:], in0=pow_mom[:], scalar1=two_beta_sq[:])
 
         h_cols = {}
+        h_rows_psum = {}
         h_rows = {}
         q_rows = {}
         grouped_tiles = {}
         code_tiles = {}
         scale_tiles = {}
+        gram_tiles = {}
+        expo_tiles = {}
+        result_tiles = {}
 
         def half_norms(b):
-            n_col = stat_pool.tile([P, ROWS], F32)
+            h_col = stat_pool.tile([P, ROWS], F32)
             for r in range(ROWS):
-                feat = psum_feat.tile([P, PACK, P], BF16, tag="feat")
+                feat = psum_stage.tile([P, PACK, P], BF16, tag="stage")
                 for t in range(PACK):
                     nc.tensor.transpose(feat[:, t, :], raw[b][:, t, P * r : P * (r + 1)], ident_bf[:])
                 squares = square_pool.tile([P, PACK, P], BF16)
-                nc.scalar.activation(out=squares[:], in_=feat[:], func=ACT.Square, accum_out=n_col[:, r : r + 1])
-            h_col = stat_pool.tile([P, ROWS], F32)
-            nc.scalar.mul(out=h_col[:], in_=n_col[:], mul=0.5)
+                nc.scalar.activation(
+                    out=squares[:], in_=feat[:], func=ACT.Square, scale=math.sqrt(0.5), accum_out=h_col[:, r : r + 1]
+                )
             h_cols[b] = h_col
 
         def spread(row, column_of):
             for r in range(ROWS):
                 nc.tensor.transpose(row[:, P * r : P * (r + 1)], column_of(r).to_broadcast([P, P]), ident_f32[:])
 
-        def rows_of(b):
-            h_row_psum = psum_rows.tile([P, N], F32)
-            spread(h_row_psum, lambda r: h_cols[b][:, r : r + 1])
+        def spread_h(b):
+            h_col = h_cols[b]
+            h_row_psum = psum_stage.tile([P, N], F32, tag="stage")
+            spread(h_row_psum, lambda r: h_col[:, r : r + 1])
+            h_rows_psum[b] = h_row_psum
+
+        def h_row_to_sbuf(b):
             h_row = stat_pool.tile([P, N], F32)
-            nc.vector.tensor_copy(out=h_row[:], in_=h_row_psum[:])
+            nc.vector.tensor_copy(out=h_row[:], in_=h_rows_psum[b][:])
             h_rows[b] = h_row
-            q_row = psum_rows.tile([P, N], F32)
+
+        def q_row_of(b):
+            q_row = psum_q.tile([P, N], F32)
             spread(q_row, lambda r: q_col[:, r, b : b + 1])
             q_rows[b] = q_row
 
         def regroup(b):
-            grouped = mx_pool.tile([P, N, PACK], BF16, align_bytes=64)
-            nc.vector.tensor_copy(
-                out=grouped[:].rearrange("p (c i) t -> p c t i", i=4),
-                in_=raw[b][:].rearrange("p t (c i) -> p c t i", i=4),
+            grouped = grouped_pool.tile([P, N, PACK], BF16, align_bytes=64)
+            nc.gpsimd.tensor_scalar(
+                out=grouped[:],
+                in0=raw[b][:].rearrange("p t n -> p n t"),
+                scalar1=1.0,
+                scalar2=0.0,
+                op0=ALU.mult,
+                op1=ALU.add,
             )
             grouped_tiles[b] = grouped
 
@@ -124,28 +139,45 @@ def tile_qcdawareold_t_kernel(tc, emb, alpha_p, beta_p, out):
             code_tiles[b] = codes
             scale_tiles[b] = scales
 
-        def weights(b):
+        def gram_of(b):
             codes, scales = code_tiles[b], scale_tiles[b]
-            expo = expo_pool.tile([P, ROWS, N], F32)
-            result = out_pool.tile([P, ROWS, N], F32)
-            diffs = {}
+            gram_0 = psum_gram.tile([P, N], F32)
+            gram_13 = psum_gram.tile([P, N], F32)
+            gram_2 = psum_gram.tile([P, N], F32)
 
-            def difference(r):
-                first = N - MOVING[r]
-                gram = psum_gram.tile([P, N], F32)
+            def product(dest, r, first, width):
                 nc.tensor.matmul_mx(
-                    out=gram[:, first:N],
+                    out=dest,
                     lhsT=codes[:, P * r : P * (r + 1)].bitcast(FP8X4),
                     lhsT_scale=scales[:, P * r : P * (r + 1)],
-                    rhs=codes[:, first:N].bitcast(FP8X4),
-                    rhs_scale=scales[:, first:N],
+                    rhs=codes[:, first : first + width].bitcast(FP8X4),
+                    rhs_scale=scales[:, first : first + width],
                     start=True,
                     stop=True,
                 )
+
+            product(gram_0[:, 0:N], 0, 0, 4 * P)
+            product(gram_13[:, P : 3 * P], 1, P, 2 * P)
+            product(gram_13[:, 3 * P : N], 1, 3 * P, P)
+            product(gram_2[:, 2 * P : N], 2, 2 * P, 2 * P)
+            product(gram_13[:, 0:P], 3, 3 * P, P)
+            gram_tiles[b] = (gram_0[:, 0:N], gram_13[:, P:N], gram_2[:, 2 * P : N], gram_13[:, 0:P])
+
+        def store(b, r):
+            nc.sync.dma_start(out=out[b, P * r : P * (r + 1), :], in_=result_tiles[b][:, r, :])
+
+        def upper_blocks(b):
+            expo = expo_pool.tile([P, ROWS, N], F32)
+            result = out_pool.tile([P, ROWS, N], F32)
+            expo_tiles[b] = expo
+            result_tiles[b] = result
+            diffs = {}
+
+            def difference(r):
                 diff = diff_pool.tile([P, N], F32)
                 nc.vector.scalar_tensor_tensor(
                     out=diff[:, P * r : N],
-                    in0=gram[:, P * r : N],
+                    in0=gram_tiles[b][r],
                     scalar=h_cols[b][:, r : r + 1],
                     in1=h_rows[b][:, P * r : N],
                     op0=ALU.subtract,
@@ -169,26 +201,38 @@ def tile_qcdawareold_t_kernel(tc, emb, alpha_p, beta_p, out):
                     difference(r)
                 if r > 0:
                     exponent(r - 1)
+            store(b, 0)
 
+        def lower_blocks(b):
+            expo, result = expo_tiles[b], result_tiles[b]
             for r in range(1, ROWS):
-                mirror = psum_mirror.tile([P, N], F32)
+                mirror = psum_stage.tile([P, N], F32, tag="stage")
                 for c in range(r):
                     nc.tensor.transpose(mirror[:, P * c : P * (c + 1)], expo[:, c, P * r : P * (r + 1)], ident_f32[:])
                 nc.scalar.activation(out=result[:, r, 0 : P * r], in_=mirror[:, 0 : P * r], func=ACT.Exp)
+                store(b, r)
 
-            nc.sync.dma_start(out=out[b].rearrange("(r p) j -> p r j", p=P), in_=result[:])
-
-        half_norms(0)
-        rows_of(0)
         regroup(0)
-        regroup(1)
+        half_norms(0)
+        spread_h(0)
         quantise(0)
+        regroup(1)
+        gram_of(0)
+        q_row_of(0)
+        h_row_to_sbuf(0)
+        half_norms(1)
         for b in range(B):
             if b + 1 < B:
-                half_norms(b + 1)
-            weights(b)
+                quantise(b + 1)
             if b + 2 < B:
                 regroup(b + 2)
+                half_norms(b + 2)
             if b + 1 < B:
-                quantise(b + 1)
-                rows_of(b + 1)
+                spread_h(b + 1)
+            upper_blocks(b)
+            if b + 1 < B:
+                gram_of(b + 1)
+            lower_blocks(b)
+            if b + 1 < B:
+                q_row_of(b + 1)
+                h_row_to_sbuf(b + 1)

@@ -15,6 +15,7 @@ ALU = mybir.AluOpType
 B, F, N = 16, 512, 512
 P = 128
 PACK = 4
+LAST = PACK - 1
 ROWS = N // P
 MOMENTUM = 4
 
@@ -31,6 +32,7 @@ def tile_qcdawareold_t_kernel(tc, emb, alpha_p, beta_p, out):
         mx_pool = ctx.enter_context(tc.tile_pool(name="mx", bufs=3))
         stat_pool = ctx.enter_context(tc.tile_pool(name="stat", bufs=4))
         square_pool = ctx.enter_context(tc.tile_pool(name="square", bufs=4))
+        last_pool = ctx.enter_context(tc.tile_pool(name="last", bufs=3))
         diff_pool = ctx.enter_context(tc.tile_pool(name="diff", bufs=4))
         expo_pool = ctx.enter_context(tc.tile_pool(name="expo", bufs=2))
         out_pool = ctx.enter_context(tc.tile_pool(name="outp", bufs=3))
@@ -40,7 +42,7 @@ def tile_qcdawareold_t_kernel(tc, emb, alpha_p, beta_p, out):
 
         mom_rows = const.tile([P, N], BF16)
         nc.vector.memset(mom_rows[:], 0.0)
-        nc.scalar.dma_start(out=mom_rows[0:B, :], in_=emb[:, MOMENTUM, :])
+        nc.sync.dma_start(out=mom_rows[0:B, :], in_=emb[:, MOMENTUM, :])
         alpha_bf = const.tile([P, 1], BF16)
         nc.scalar.dma_start(out=alpha_bf[:], in_=alpha_p.rearrange("a b -> (a b)").partition_broadcast(P))
         beta_bf = const.tile([P, 1], BF16)
@@ -56,6 +58,8 @@ def tile_qcdawareold_t_kernel(tc, emb, alpha_p, beta_p, out):
         make_identity(nc, ident_bf[:])
         ident_f32 = const.tile([P, P], F32)
         make_identity(nc, ident_f32[:])
+        ones = const.tile([P, 2], F32)
+        nc.vector.memset(ones[:], 1.0)
 
         two_alpha = const.tile([P, 1], F32)
         nc.vector.tensor_scalar_mul(out=two_alpha[:], in0=alpha_bf[:], scalar1=2.0)
@@ -73,6 +77,9 @@ def tile_qcdawareold_t_kernel(tc, emb, alpha_p, beta_p, out):
         q_col = const.tile([P, ROWS, B], F32)
         nc.vector.tensor_scalar_mul(out=q_col[:], in0=pow_mom[:], scalar1=two_beta_sq[:])
 
+        last_squares = {}
+        most_parts = {}
+        rest_parts = {}
         h_cols = {}
         h_rows_psum = {}
         h_rows = {}
@@ -84,16 +91,34 @@ def tile_qcdawareold_t_kernel(tc, emb, alpha_p, beta_p, out):
         expo_tiles = {}
         result_tiles = {}
 
+        def square_last(b):
+            last_sq = last_pool.tile([P, N], F32)
+            nc.gpsimd.tensor_tensor(out=last_sq[:], in0=raw[b][:, LAST, :], in1=raw[b][:, LAST, :], op=ALU.mult)
+            last_squares[b] = last_sq
+
+        def partial_norms(b):
+            most = stat_pool.tile([P, ROWS], F32)
+            for r in range(ROWS):
+                feat = psum_stage.tile([P, LAST, P], BF16, tag="stage")
+                for t in range(LAST):
+                    nc.tensor.transpose(feat[:, t, :], raw[b][:, t, P * r : P * (r + 1)], ident_bf[:])
+                squares = square_pool.tile([P, LAST, P], BF16)
+                nc.scalar.activation(
+                    out=squares[:], in_=feat[:], func=ACT.Square, scale=math.sqrt(0.5), accum_out=most[:, r : r + 1]
+                )
+            rest = psum_stage.tile([P, ROWS, 2], F32, tag="stage")
+            for r in range(ROWS):
+                nc.tensor.matmul(
+                    out=rest[:, r, :], lhsT=last_squares[b][:, P * r : P * (r + 1)], rhs=ones[:], start=True, stop=True
+                )
+            most_parts[b] = most
+            rest_parts[b] = rest
+
         def half_norms(b):
             h_col = stat_pool.tile([P, ROWS], F32)
-            for r in range(ROWS):
-                feat = psum_stage.tile([P, PACK, P], BF16, tag="stage")
-                for t in range(PACK):
-                    nc.tensor.transpose(feat[:, t, :], raw[b][:, t, P * r : P * (r + 1)], ident_bf[:])
-                squares = square_pool.tile([P, PACK, P], BF16)
-                nc.scalar.activation(
-                    out=squares[:], in_=feat[:], func=ACT.Square, scale=math.sqrt(0.5), accum_out=h_col[:, r : r + 1]
-                )
+            nc.vector.scalar_tensor_tensor(
+                out=h_col[:], in0=rest_parts[b][:, :, 0], scalar=0.5, in1=most_parts[b][:], op0=ALU.mult, op1=ALU.add
+            )
             h_cols[b] = h_col
 
         def spread(row, column_of):
@@ -212,24 +237,34 @@ def tile_qcdawareold_t_kernel(tc, emb, alpha_p, beta_p, out):
                 nc.scalar.activation(out=result[:, r, 0 : P * r], in_=mirror[:, 0 : P * r], func=ACT.Exp)
                 store(b, r)
 
+        square_last(0)
         regroup(0)
-        half_norms(0)
-        spread_h(0)
+        square_last(1)
+        partial_norms(0)
         quantise(0)
         regroup(1)
+        square_last(2)
+        half_norms(0)
+        spread_h(0)
         gram_of(0)
         q_row_of(0)
         h_row_to_sbuf(0)
+        partial_norms(1)
         half_norms(1)
         for b in range(B):
             if b + 1 < B:
                 quantise(b + 1)
             if b + 2 < B:
                 regroup(b + 2)
-                half_norms(b + 2)
+            if b + 3 < B:
+                square_last(b + 3)
+            if b + 2 < B:
+                partial_norms(b + 2)
             if b + 1 < B:
                 spread_h(b + 1)
             upper_blocks(b)
+            if b + 2 < B:
+                half_norms(b + 2)
             if b + 1 < B:
                 gram_of(b + 1)
             lower_blocks(b)

@@ -15,9 +15,9 @@ ALU = mybir.AluOpType
 B, F, N = 16, 512, 512
 P = 128
 PACK = 4
-LAST = PACK - 1
 ROWS = N // P
 MOMENTUM = 4
+MOVING = (512, 512, 256, 128)
 
 FLOPS = 2 * B * N * N * F
 
@@ -32,7 +32,6 @@ def tile_qcdawareold_t_kernel(tc, emb, alpha_p, beta_p, out):
         mx_pool = ctx.enter_context(tc.tile_pool(name="mx", bufs=3))
         stat_pool = ctx.enter_context(tc.tile_pool(name="stat", bufs=4))
         square_pool = ctx.enter_context(tc.tile_pool(name="square", bufs=4))
-        last_pool = ctx.enter_context(tc.tile_pool(name="last", bufs=3))
         diff_pool = ctx.enter_context(tc.tile_pool(name="diff", bufs=4))
         expo_pool = ctx.enter_context(tc.tile_pool(name="expo", bufs=2))
         out_pool = ctx.enter_context(tc.tile_pool(name="outp", bufs=3))
@@ -58,8 +57,6 @@ def tile_qcdawareold_t_kernel(tc, emb, alpha_p, beta_p, out):
         make_identity(nc, ident_bf[:])
         ident_f32 = const.tile([P, P], F32)
         make_identity(nc, ident_f32[:])
-        ones = const.tile([P, 2], F32)
-        nc.vector.memset(ones[:], 1.0)
 
         two_alpha = const.tile([P, 1], F32)
         nc.vector.tensor_scalar_mul(out=two_alpha[:], in0=alpha_bf[:], scalar1=2.0)
@@ -77,9 +74,6 @@ def tile_qcdawareold_t_kernel(tc, emb, alpha_p, beta_p, out):
         q_col = const.tile([P, ROWS, B], F32)
         nc.vector.tensor_scalar_mul(out=q_col[:], in0=pow_mom[:], scalar1=two_beta_sq[:])
 
-        last_squares = {}
-        most_parts = {}
-        rest_parts = {}
         h_cols = {}
         h_rows_psum = {}
         h_rows = {}
@@ -91,34 +85,16 @@ def tile_qcdawareold_t_kernel(tc, emb, alpha_p, beta_p, out):
         expo_tiles = {}
         result_tiles = {}
 
-        def square_last(b):
-            last_sq = last_pool.tile([P, N], F32)
-            nc.gpsimd.tensor_tensor(out=last_sq[:], in0=raw[b][:, LAST, :], in1=raw[b][:, LAST, :], op=ALU.mult)
-            last_squares[b] = last_sq
-
-        def partial_norms(b):
-            most = stat_pool.tile([P, ROWS], F32)
-            for r in range(ROWS):
-                feat = psum_stage.tile([P, LAST, P], BF16, tag="stage")
-                for t in range(LAST):
-                    nc.tensor.transpose(feat[:, t, :], raw[b][:, t, P * r : P * (r + 1)], ident_bf[:])
-                squares = square_pool.tile([P, LAST, P], BF16)
-                nc.scalar.activation(
-                    out=squares[:], in_=feat[:], func=ACT.Square, scale=math.sqrt(0.5), accum_out=most[:, r : r + 1]
-                )
-            rest = psum_stage.tile([P, ROWS, 2], F32, tag="stage")
-            for r in range(ROWS):
-                nc.tensor.matmul(
-                    out=rest[:, r, :], lhsT=last_squares[b][:, P * r : P * (r + 1)], rhs=ones[:], start=True, stop=True
-                )
-            most_parts[b] = most
-            rest_parts[b] = rest
-
         def half_norms(b):
             h_col = stat_pool.tile([P, ROWS], F32)
-            nc.vector.scalar_tensor_tensor(
-                out=h_col[:], in0=rest_parts[b][:, :, 0], scalar=0.5, in1=most_parts[b][:], op0=ALU.mult, op1=ALU.add
-            )
+            for r in range(ROWS):
+                feat = psum_stage.tile([P, PACK, P], BF16, tag="stage")
+                for t in range(PACK):
+                    nc.tensor.transpose(feat[:, t, :], raw[b][:, t, P * r : P * (r + 1)], ident_bf[:])
+                squares = square_pool.tile([P, PACK, P], BF16)
+                nc.scalar.activation(
+                    out=squares[:], in_=feat[:], func=ACT.Square, scale=math.sqrt(0.5), accum_out=h_col[:, r : r + 1]
+                )
             h_cols[b] = h_col
 
         def spread(row, column_of):
@@ -167,26 +143,21 @@ def tile_qcdawareold_t_kernel(tc, emb, alpha_p, beta_p, out):
         def gram_of(b):
             codes, scales = code_tiles[b], scale_tiles[b]
             gram_0 = psum_gram.tile([P, N], F32)
-            gram_13 = psum_gram.tile([P, N], F32)
-            gram_2 = psum_gram.tile([P, N], F32)
-
-            def product(dest, r, first, width):
+            gram_1 = psum_gram.tile([P, N], F32)
+            gram_23 = psum_gram.tile([P, N], F32)
+            homes = (gram_0[:, 0:N], gram_1[:, 0:N], gram_23[:, 2 * P : N], gram_23[:, 0:P])
+            for r in range(ROWS):
+                first = N - MOVING[r]
                 nc.tensor.matmul_mx(
-                    out=dest,
+                    out=homes[r],
                     lhsT=codes[:, P * r : P * (r + 1)].bitcast(FP8X4),
                     lhsT_scale=scales[:, P * r : P * (r + 1)],
-                    rhs=codes[:, first : first + width].bitcast(FP8X4),
-                    rhs_scale=scales[:, first : first + width],
+                    rhs=codes[:, first:N].bitcast(FP8X4),
+                    rhs_scale=scales[:, first:N],
                     start=True,
                     stop=True,
                 )
-
-            product(gram_0[:, 0:N], 0, 0, 4 * P)
-            product(gram_13[:, P : 3 * P], 1, P, 2 * P)
-            product(gram_13[:, 3 * P : N], 1, 3 * P, P)
-            product(gram_2[:, 2 * P : N], 2, 2 * P, 2 * P)
-            product(gram_13[:, 0:P], 3, 3 * P, P)
-            gram_tiles[b] = (gram_0[:, 0:N], gram_13[:, P:N], gram_2[:, 2 * P : N], gram_13[:, 0:P])
+            gram_tiles[b] = (gram_0[:, 0:N], gram_1[:, P:N], gram_23[:, 2 * P : N], gram_23[:, 0:P])
 
         def store(b, r):
             nc.sync.dma_start(out=out[b, P * r : P * (r + 1), :], in_=result_tiles[b][:, r, :])
@@ -237,34 +208,24 @@ def tile_qcdawareold_t_kernel(tc, emb, alpha_p, beta_p, out):
                 nc.scalar.activation(out=result[:, r, 0 : P * r], in_=mirror[:, 0 : P * r], func=ACT.Exp)
                 store(b, r)
 
-        square_last(0)
         regroup(0)
-        square_last(1)
-        partial_norms(0)
+        half_norms(0)
+        half_norms(1)
+        spread_h(0)
         quantise(0)
         regroup(1)
-        square_last(2)
-        half_norms(0)
-        spread_h(0)
+        h_row_to_sbuf(0)
         gram_of(0)
         q_row_of(0)
-        h_row_to_sbuf(0)
-        partial_norms(1)
-        half_norms(1)
         for b in range(B):
             if b + 1 < B:
                 quantise(b + 1)
             if b + 2 < B:
                 regroup(b + 2)
-            if b + 3 < B:
-                square_last(b + 3)
-            if b + 2 < B:
-                partial_norms(b + 2)
+                half_norms(b + 2)
             if b + 1 < B:
                 spread_h(b + 1)
             upper_blocks(b)
-            if b + 2 < B:
-                half_norms(b + 2)
             if b + 1 < B:
                 gram_of(b + 1)
             lower_blocks(b)

@@ -28,7 +28,7 @@ def tile_qcdawareold_t_kernel(tc, emb, alpha_p, beta_p, out):
         ctx.enter_context(tc.manual_schedule())
         const = ctx.enter_context(tc.tile_pool(name="const", bufs=1))
         raw_pool = ctx.enter_context(tc.tile_pool(name="raw", bufs=B))
-        grouped_pool = ctx.enter_context(tc.tile_pool(name="grouped", bufs=1))
+        grouped_pool = ctx.enter_context(tc.tile_pool(name="grouped", bufs=2))
         mx_pool = ctx.enter_context(tc.tile_pool(name="mx", bufs=3))
         stat_pool = ctx.enter_context(tc.tile_pool(name="stat", bufs=4))
         square_pool = ctx.enter_context(tc.tile_pool(name="square", bufs=4))
@@ -119,13 +119,9 @@ def tile_qcdawareold_t_kernel(tc, emb, alpha_p, beta_p, out):
 
         def regroup(b):
             grouped = grouped_pool.tile([P, N, PACK], BF16, align_bytes=64)
-            nc.gpsimd.tensor_scalar(
-                out=grouped[:],
-                in0=raw[b][:].rearrange("p t n -> p n t"),
-                scalar1=1.0,
-                scalar2=0.0,
-                op0=ALU.mult,
-                op1=ALU.add,
+            nc.vector.tensor_copy(
+                out=grouped[:].rearrange("p (c i) t -> p c t i", i=4),
+                in_=raw[b][:].rearrange("p t (c i) -> p c t i", i=4),
             )
             grouped_tiles[b] = grouped
 
@@ -211,9 +207,9 @@ def tile_qcdawareold_t_kernel(tc, emb, alpha_p, beta_p, out):
         regroup(0)
         half_norms(0)
         half_norms(1)
-        spread_h(0)
-        quantise(0)
         regroup(1)
+        quantise(0)
+        spread_h(0)
         h_row_to_sbuf(0)
         gram_of(0)
         q_row_of(0)
@@ -221,11 +217,12 @@ def tile_qcdawareold_t_kernel(tc, emb, alpha_p, beta_p, out):
             if b + 1 < B:
                 quantise(b + 1)
             if b + 2 < B:
-                regroup(b + 2)
                 half_norms(b + 2)
             if b + 1 < B:
                 spread_h(b + 1)
             upper_blocks(b)
+            if b + 2 < B:
+                regroup(b + 2)
             if b + 1 < B:
                 gram_of(b + 1)
             lower_blocks(b)

@@ -28,13 +28,13 @@ def tile_qcdawareold_t_kernel(tc, emb, alpha_p, beta_p, out):
         ctx.enter_context(tc.manual_schedule())
         const = ctx.enter_context(tc.tile_pool(name="const", bufs=1))
         raw_pool = ctx.enter_context(tc.tile_pool(name="raw", bufs=B))
-        grouped_pool = ctx.enter_context(tc.tile_pool(name="grouped", bufs=2))
+        grouped_pool = ctx.enter_context(tc.tile_pool(name="grouped", bufs=1))
         mx_pool = ctx.enter_context(tc.tile_pool(name="mx", bufs=3))
         stat_pool = ctx.enter_context(tc.tile_pool(name="stat", bufs=4))
         square_pool = ctx.enter_context(tc.tile_pool(name="square", bufs=4))
         diff_pool = ctx.enter_context(tc.tile_pool(name="diff", bufs=4))
         expo_pool = ctx.enter_context(tc.tile_pool(name="expo", bufs=2))
-        out_pool = ctx.enter_context(tc.tile_pool(name="outp", bufs=3))
+        out_pool = ctx.enter_context(tc.tile_pool(name="outp", bufs=4))
         psum_gram = ctx.enter_context(tc.psum_pool(name="psum_gram", bufs=1))
         psum_q = ctx.enter_context(tc.psum_pool(name="psum_q", bufs=1))
         psum_stage = ctx.enter_context(tc.psum_pool(name="psum_stage", bufs=4))
@@ -84,6 +84,7 @@ def tile_qcdawareold_t_kernel(tc, emb, alpha_p, beta_p, out):
         gram_tiles = {}
         expo_tiles = {}
         result_tiles = {}
+        mirror_tiles = {}
 
         def half_norms(b):
             h_col = stat_pool.tile([P, ROWS], F32)
@@ -119,9 +120,13 @@ def tile_qcdawareold_t_kernel(tc, emb, alpha_p, beta_p, out):
 
         def regroup(b):
             grouped = grouped_pool.tile([P, N, PACK], BF16, align_bytes=64)
-            nc.vector.tensor_copy(
-                out=grouped[:].rearrange("p (c i) t -> p c t i", i=4),
-                in_=raw[b][:].rearrange("p t (c i) -> p c t i", i=4),
+            nc.gpsimd.tensor_scalar(
+                out=grouped[:],
+                in0=raw[b][:].rearrange("p t n -> p n t"),
+                scalar1=1.0,
+                scalar2=0.0,
+                op0=ALU.mult,
+                op1=ALU.add,
             )
             grouped_tiles[b] = grouped
 
@@ -195,21 +200,35 @@ def tile_qcdawareold_t_kernel(tc, emb, alpha_p, beta_p, out):
                     exponent(r - 1)
             store(b, 0)
 
-        def lower_blocks(b):
+        def lower_rows_1_2(b):
             expo, result = expo_tiles[b], result_tiles[b]
-            for r in range(1, ROWS):
+            for r in range(1, ROWS - 1):
                 mirror = psum_stage.tile([P, N], F32, tag="stage")
                 for c in range(r):
                     nc.tensor.transpose(mirror[:, P * c : P * (c + 1)], expo[:, c, P * r : P * (r + 1)], ident_f32[:])
                 nc.scalar.activation(out=result[:, r, 0 : P * r], in_=mirror[:, 0 : P * r], func=ACT.Exp)
                 store(b, r)
 
+        def transpose_into_row_3(b):
+            r = ROWS - 1
+            mirror = psum_stage.tile([P, N], F32, tag="stage")
+            for c in range(r):
+                nc.tensor.transpose(
+                    mirror[:, P * c : P * (c + 1)], result_tiles[b][:, c, P * r : P * (r + 1)], ident_f32[:]
+                )
+            mirror_tiles[b] = mirror
+
+        def copy_into_row_3(b):
+            r = ROWS - 1
+            nc.vector.tensor_copy(out=result_tiles[b][:, r, 0 : P * r], in_=mirror_tiles[b][:, 0 : P * r])
+            store(b, r)
+
         regroup(0)
         half_norms(0)
         half_norms(1)
-        regroup(1)
-        quantise(0)
         spread_h(0)
+        quantise(0)
+        regroup(1)
         h_row_to_sbuf(0)
         gram_of(0)
         q_row_of(0)
@@ -217,15 +236,20 @@ def tile_qcdawareold_t_kernel(tc, emb, alpha_p, beta_p, out):
             if b + 1 < B:
                 quantise(b + 1)
             if b + 2 < B:
+                regroup(b + 2)
                 half_norms(b + 2)
+            if b > 0:
+                transpose_into_row_3(b - 1)
             if b + 1 < B:
                 spread_h(b + 1)
             upper_blocks(b)
-            if b + 2 < B:
-                regroup(b + 2)
+            if b > 0:
+                copy_into_row_3(b - 1)
             if b + 1 < B:
                 gram_of(b + 1)
-            lower_blocks(b)
+            lower_rows_1_2(b)
             if b + 1 < B:
                 q_row_of(b + 1)
                 h_row_to_sbuf(b + 1)
+        transpose_into_row_3(B - 1)
+        copy_into_row_3(B - 1)

@@ -75,6 +75,8 @@ def tile_qcdawareold_t_kernel(tc, emb, alpha_p, beta_p, out):
         nc.vector.tensor_scalar_mul(out=q_col[:], in0=pow_mom[:], scalar1=two_beta_sq[:])
 
         h_cols = {}
+        feature_tiles = {}
+        square_grams = {}
         h_rows_psum = {}
         h_rows = {}
         q_rows = {}
@@ -82,21 +84,48 @@ def tile_qcdawareold_t_kernel(tc, emb, alpha_p, beta_p, out):
         code_tiles = {}
         scale_tiles = {}
         gram_tiles = {}
+        flipped_tiles = {}
+        diffs = {}
         expo_tiles = {}
         result_tiles = {}
-        mirror_tiles = {}
 
-        def half_norms(b):
-            h_col = stat_pool.tile([P, ROWS], F32)
-            for r in range(ROWS):
-                feat = psum_stage.tile([P, PACK, P], BF16, tag="stage")
-                for t in range(PACK):
-                    nc.tensor.transpose(feat[:, t, :], raw[b][:, t, P * r : P * (r + 1)], ident_bf[:])
-                squares = square_pool.tile([P, PACK, P], BF16)
-                nc.scalar.activation(
-                    out=squares[:], in_=feat[:], func=ACT.Square, scale=math.sqrt(0.5), accum_out=h_col[:, r : r + 1]
-                )
-            h_cols[b] = h_col
+        def features(b, r):
+            feat = psum_stage.tile([P, PACK, P], BF16, tag="stage")
+            for t in range(PACK):
+                nc.tensor.transpose(feat[:, t, :], raw[b][:, t, P * r : P * (r + 1)], ident_bf[:])
+            feature_tiles[b, r] = feat
+
+        def sum_squares(b, r):
+            squares = square_pool.tile([P, PACK, P], BF16)
+            nc.scalar.activation(
+                out=squares[:],
+                in_=feature_tiles[b, r][:],
+                func=ACT.Square,
+                scale=math.sqrt(0.5),
+                accum_out=h_cols[b][:, r : r + 1],
+            )
+
+        def open_norms(b):
+            h_cols[b] = stat_pool.tile([P, ROWS], F32, name="h_col")
+
+        def square_gram(b, r):
+            gram = psum_stage.tile([P, P], F32, tag="stage")
+            for t in range(PACK):
+                block = raw[b][:, t, P * r : P * (r + 1)]
+                nc.tensor.matmul(gram[:], lhsT=block, rhs=block, start=(t == 0), stop=(t == PACK - 1))
+            square_grams[b, r] = gram
+
+        def sum_diagonal(b, r):
+            diagonal = square_pool.tile([P, P], F32)
+            nc.vector.scalar_tensor_tensor(
+                out=diagonal[:],
+                in0=square_grams[b, r][:],
+                scalar=0.5,
+                in1=ident_f32[:],
+                op0=ALU.mult,
+                op1=ALU.mult,
+                accum_out=h_cols[b][:, r : r + 1],
+            )
 
         def spread(row, column_of):
             for r in range(ROWS):
@@ -163,93 +192,117 @@ def tile_qcdawareold_t_kernel(tc, emb, alpha_p, beta_p, out):
         def store(b, r):
             nc.sync.dma_start(out=out[b, P * r : P * (r + 1), :], in_=result_tiles[b][:, r, :])
 
-        def upper_blocks(b):
-            expo = expo_pool.tile([P, ROWS, N], F32)
-            result = out_pool.tile([P, ROWS, N], F32)
-            expo_tiles[b] = expo
-            result_tiles[b] = result
-            diffs = {}
+        def open_batch(b):
+            expo_tiles[b] = expo_pool.tile([P, ROWS, N], F32, name="expo")
+            result_tiles[b] = out_pool.tile([P, ROWS, N], F32, name="result")
 
-            def difference(r):
-                diff = diff_pool.tile([P, N], F32)
-                nc.vector.scalar_tensor_tensor(
-                    out=diff[:, P * r : N],
-                    in0=gram_tiles[b][r],
-                    scalar=h_cols[b][:, r : r + 1],
-                    in1=h_rows[b][:, P * r : N],
-                    op0=ALU.subtract,
-                    op1=ALU.subtract,
-                )
-                diffs[r] = diff
+        def difference(b, r):
+            diff = diff_pool.tile([P, N], F32)
+            nc.vector.scalar_tensor_tensor(
+                out=diff[:, P * r : N],
+                in0=gram_tiles[b][r],
+                scalar=h_cols[b][:, r : r + 1],
+                in1=h_rows[b][:, P * r : N],
+                op0=ALU.subtract,
+                op1=ALU.subtract,
+            )
+            diffs[r] = diff
 
-            def exponent(r):
-                nc.vector.scalar_tensor_tensor(
-                    out=expo[:, r, P * r : N],
-                    in0=q_rows[b][:, P * r : N],
-                    scalar=q_col[:, r, b : b + 1],
-                    in1=diffs[r][:, P * r : N],
-                    op0=ALU.min,
-                    op1=ALU.mult,
-                )
-                nc.scalar.activation(out=result[:, r, P * r : N], in_=expo[:, r, P * r : N], func=ACT.Exp)
+        def exponent(b, r):
+            nc.vector.scalar_tensor_tensor(
+                out=expo_tiles[b][:, r, P * r : N],
+                in0=q_rows[b][:, P * r : N],
+                scalar=q_col[:, r, b : b + 1],
+                in1=diffs[r][:, P * r : N],
+                op0=ALU.min,
+                op1=ALU.mult,
+            )
 
-            for r in range(ROWS + 1):
-                if r < ROWS:
-                    difference(r)
-                if r > 0:
-                    exponent(r - 1)
-            store(b, 0)
+        def upper_row(b, r):
+            nc.scalar.activation(
+                out=result_tiles[b][:, r, P * r : N], in_=expo_tiles[b][:, r, P * r : N], func=ACT.Exp
+            )
 
-        def lower_rows_1_2(b):
-            expo, result = expo_tiles[b], result_tiles[b]
-            for r in range(1, ROWS - 1):
-                mirror = psum_stage.tile([P, N], F32, tag="stage")
-                for c in range(r):
-                    nc.tensor.transpose(mirror[:, P * c : P * (c + 1)], expo[:, c, P * r : P * (r + 1)], ident_f32[:])
-                nc.scalar.activation(out=result[:, r, 0 : P * r], in_=mirror[:, 0 : P * r], func=ACT.Exp)
-                store(b, r)
+        def mirror(b, c):
+            below = ROWS - 1 - c
+            flipped = psum_stage.tile([P, below, P], F32, tag="stage")
+            for k in range(below):
+                r = c + 1 + k
+                nc.tensor.transpose(flipped[:, k, :], expo_tiles[b][:, c, P * r : P * (r + 1)], ident_f32[:])
+            flipped_tiles[b, c] = flipped
 
-        def transpose_into_row_3(b):
-            r = ROWS - 1
-            mirror = psum_stage.tile([P, N], F32, tag="stage")
-            for c in range(r):
-                nc.tensor.transpose(
-                    mirror[:, P * c : P * (c + 1)], result_tiles[b][:, c, P * r : P * (r + 1)], ident_f32[:]
-                )
-            mirror_tiles[b] = mirror
+        def lower_column(b, c):
+            nc.scalar.activation(
+                out=result_tiles[b][:, c + 1 : ROWS, P * c : P * (c + 1)], in_=flipped_tiles[b, c][:], func=ACT.Exp
+            )
 
-        def copy_into_row_3(b):
-            r = ROWS - 1
-            nc.vector.tensor_copy(out=result_tiles[b][:, r, 0 : P * r], in_=mirror_tiles[b][:, 0 : P * r])
-            store(b, r)
-
-        regroup(0)
-        half_norms(0)
-        half_norms(1)
-        spread_h(0)
+        first_grouped = grouped_pool.tile([P, N, PACK], BF16, align_bytes=64, name="grouped")
+        nc.vector.tensor_copy(out=first_grouped[:], in_=raw[0][:].rearrange("p t n -> p n t"))
+        grouped_tiles[0] = first_grouped
+        open_norms(0)
+        for r in range(ROWS - 1, 0, -1):
+            square_gram(0, r)
+        features(0, 0)
+        sum_squares(0, 0)
+        for r in range(ROWS - 1, 0, -1):
+            sum_diagonal(0, r)
+        open_norms(1)
+        square_gram(1, ROWS - 1)
+        for r in range(ROWS - 1):
+            features(1, r)
+            sum_squares(1, r)
         quantise(0)
-        regroup(1)
+        spread_h(0)
         h_row_to_sbuf(0)
+        sum_diagonal(1, ROWS - 1)
+        regroup(1)
         gram_of(0)
         q_row_of(0)
         for b in range(B):
-            if b + 1 < B:
-                quantise(b + 1)
-            if b + 2 < B:
-                regroup(b + 2)
-                half_norms(b + 2)
-            if b > 0:
-                transpose_into_row_3(b - 1)
-            if b + 1 < B:
+            more_1 = b + 1 < B
+            more_2 = b + 2 < B
+            open_batch(b)
+            difference(b, 0)
+            difference(b, 1)
+            exponent(b, 0)
+            if more_2:
+                open_norms(b + 2)
+                square_gram(b + 2, ROWS - 1)
+                features(b + 2, 0)
+                sum_squares(b + 2, 0)
+            upper_row(b, 0)
+            store(b, 0)
+            mirror(b, 0)
+            lower_column(b, 0)
+            difference(b, 2)
+            if more_1:
                 spread_h(b + 1)
-            upper_blocks(b)
-            if b > 0:
-                copy_into_row_3(b - 1)
-            if b + 1 < B:
-                gram_of(b + 1)
-            lower_rows_1_2(b)
-            if b + 1 < B:
-                q_row_of(b + 1)
+            if more_2:
+                sum_diagonal(b + 2, ROWS - 1)
+                features(b + 2, 1)
+                sum_squares(b + 2, 1)
+            exponent(b, 1)
+            upper_row(b, 1)
+            mirror(b, 1)
+            lower_column(b, 1)
+            store(b, 1)
+            difference(b, 3)
+            if more_1:
+                quantise(b + 1)
                 h_row_to_sbuf(b + 1)
-        transpose_into_row_3(B - 1)
-        copy_into_row_3(B - 1)
+            if more_2:
+                regroup(b + 2)
+                features(b + 2, 2)
+                sum_squares(b + 2, 2)
+            if more_1:
+                gram_of(b + 1)
+            exponent(b, 2)
+            upper_row(b, 2)
+            mirror(b, 2)
+            lower_column(b, 2)
+            store(b, 2)
+            exponent(b, 3)
+            upper_row(b, 3)
+            store(b, 3)
+            if more_1:
+                q_row_of(b + 1)

@@ -19,6 +19,8 @@ ROWS = N // P
 MOMENTUM = 4
 MOVING = (512, 512, 256, 128)
 
+HALVES = (slice(0, N // 2), slice(N // 2, N))
+
 FLOPS = 2 * B * N * N * F
 
 
@@ -50,7 +52,10 @@ def tile_qcdawareold_t_kernel(tc, emb, alpha_p, beta_p, out):
         raw = []
         for b in range(B):
             e_raw = raw_pool.tile([P, PACK, N], BF16)
-            nc.sync.dma_start(out=e_raw[:], in_=emb[b].rearrange("(p t) n -> p t n", t=PACK))
+            features_of_b = emb[b].rearrange("(p t) n -> p t n", t=PACK)
+            pieces = HALVES if b == 0 else (slice(0, N),)
+            for piece in pieces:
+                nc.sync.dma_start(out=e_raw[:, :, piece], in_=features_of_b[:, :, piece])
             raw.append(e_raw)
 
         ident_bf = const.tile([P, P], BF16)
@@ -72,7 +77,9 @@ def tile_qcdawareold_t_kernel(tc, emb, alpha_p, beta_p, out):
         pow_mom = const.tile([P, ROWS, B], F32)
         nc.scalar.activation(out=pow_mom[:], in_=log_mom[:], func=ACT.Exp, scale=two_alpha[:])
         q_col = const.tile([P, ROWS, B], F32)
-        nc.vector.tensor_scalar_mul(out=q_col[:], in0=pow_mom[:], scalar1=two_beta_sq[:])
+        nc.gpsimd.tensor_scalar(
+            out=q_col[:], in0=pow_mom[:], scalar1=two_beta_sq[:], scalar2=0.0, op0=ALU.mult, op1=ALU.add
+        )
 
         h_cols = {}
         feature_tiles = {}
@@ -83,6 +90,7 @@ def tile_qcdawareold_t_kernel(tc, emb, alpha_p, beta_p, out):
         grouped_tiles = {}
         code_tiles = {}
         scale_tiles = {}
+        gram_homes = {}
         gram_tiles = {}
         flipped_tiles = {}
         diffs = {}
@@ -170,16 +178,19 @@ def tile_qcdawareold_t_kernel(tc, emb, alpha_p, beta_p, out):
             code_tiles[b] = codes
             scale_tiles[b] = scales
 
-        def gram_of(b):
-            codes, scales = code_tiles[b], scale_tiles[b]
+        def open_gram(b):
             gram_0 = psum_gram.tile([P, N], F32)
             gram_1 = psum_gram.tile([P, N], F32)
             gram_23 = psum_gram.tile([P, N], F32)
-            homes = (gram_0[:, 0:N], gram_1[:, 0:N], gram_23[:, 2 * P : N], gram_23[:, 0:P])
-            for r in range(ROWS):
+            gram_homes[b] = (gram_0[:, 0:N], gram_1[:, 0:N], gram_23[:, 2 * P : N], gram_23[:, 0:P])
+            gram_tiles[b] = (gram_0[:, 0:N], gram_1[:, P:N], gram_23[:, 2 * P : N], gram_23[:, 0:P])
+
+        def gram_rows(b, rows):
+            codes, scales = code_tiles[b], scale_tiles[b]
+            for r in rows:
                 first = N - MOVING[r]
                 nc.tensor.matmul_mx(
-                    out=homes[r],
+                    out=gram_homes[b][r],
                     lhsT=codes[:, P * r : P * (r + 1)].bitcast(FP8X4),
                     lhsT_scale=scales[:, P * r : P * (r + 1)],
                     rhs=codes[:, first:N].bitcast(FP8X4),
@@ -187,7 +198,6 @@ def tile_qcdawareold_t_kernel(tc, emb, alpha_p, beta_p, out):
                     start=True,
                     stop=True,
                 )
-            gram_tiles[b] = (gram_0[:, 0:N], gram_1[:, P:N], gram_23[:, 2 * P : N], gram_23[:, 0:P])
 
         def store(b, r):
             nc.sync.dma_start(out=out[b, P * r : P * (r + 1), :], in_=result_tiles[b][:, r, :])
@@ -237,27 +247,28 @@ def tile_qcdawareold_t_kernel(tc, emb, alpha_p, beta_p, out):
             )
 
         first_grouped = grouped_pool.tile([P, N, PACK], BF16, align_bytes=64, name="grouped")
-        nc.vector.tensor_copy(out=first_grouped[:], in_=raw[0][:].rearrange("p t n -> p n t"))
+        for half in HALVES:
+            nc.vector.tensor_copy(out=first_grouped[:, half, :], in_=raw[0][:, :, half].rearrange("p t n -> p n t"))
         grouped_tiles[0] = first_grouped
         open_norms(0)
-        for r in range(ROWS - 1, 0, -1):
-            square_gram(0, r)
+        quantise(0)
         features(0, 0)
         sum_squares(0, 0)
-        for r in range(ROWS - 1, 0, -1):
+        for r in (1, 2, 3):
+            square_gram(0, r)
             sum_diagonal(0, r)
-        open_norms(1)
-        square_gram(1, ROWS - 1)
-        for r in range(ROWS - 1):
-            features(1, r)
-            sum_squares(1, r)
-        quantise(0)
         spread_h(0)
         h_row_to_sbuf(0)
-        sum_diagonal(1, ROWS - 1)
         regroup(1)
-        gram_of(0)
+        open_gram(0)
+        gram_rows(0, (0, 1, 2, 3))
         q_row_of(0)
+        open_norms(1)
+        for r in (0, 1):
+            features(1, r)
+            sum_squares(1, r)
+        for r in (2, 3):
+            square_gram(1, r)
         for b in range(B):
             more_1 = b + 1 < B
             more_2 = b + 2 < B
@@ -275,34 +286,40 @@ def tile_qcdawareold_t_kernel(tc, emb, alpha_p, beta_p, out):
             mirror(b, 0)
             lower_column(b, 0)
             difference(b, 2)
+            if b == 0:
+                for r in (2, 3):
+                    sum_diagonal(1, r)
             if more_1:
+                quantise(b + 1)
                 spread_h(b + 1)
             if more_2:
+                regroup(b + 2)
                 sum_diagonal(b + 2, ROWS - 1)
                 features(b + 2, 1)
                 sum_squares(b + 2, 1)
             exponent(b, 1)
+            if more_1:
+                open_gram(b + 1)
+                gram_rows(b + 1, (0, 1))
             upper_row(b, 1)
             mirror(b, 1)
             lower_column(b, 1)
             store(b, 1)
             difference(b, 3)
             if more_1:
-                quantise(b + 1)
                 h_row_to_sbuf(b + 1)
             if more_2:
-                regroup(b + 2)
                 features(b + 2, 2)
                 sum_squares(b + 2, 2)
             if more_1:
-                gram_of(b + 1)
+                gram_rows(b + 1, (2, 3))
             exponent(b, 2)
             upper_row(b, 2)
-            mirror(b, 2)
-            lower_column(b, 2)
             store(b, 2)
+            mirror(b, 2)
             exponent(b, 3)
             upper_row(b, 3)
+            lower_column(b, 2)
             store(b, 3)
             if more_1:
                 q_row_of(b + 1)

@@ -300,7 +300,6 @@ def tile_qcdawareold_t_kernel(tc, emb, alpha_p, beta_p, out):
             exponent(b, 1)
             if more_1:
                 open_gram(b + 1)
-                gram_rows(b + 1, (0, 1))
             upper_row(b, 1)
             mirror(b, 1)
             lower_column(b, 1)
@@ -308,18 +307,17 @@ def tile_qcdawareold_t_kernel(tc, emb, alpha_p, beta_p, out):
             difference(b, 3)
             if more_1:
                 h_row_to_sbuf(b + 1)
+                gram_rows(b + 1, (0, 1, 2, 3))
             if more_2:
                 features(b + 2, 2)
                 sum_squares(b + 2, 2)
-            if more_1:
-                gram_rows(b + 1, (2, 3))
             exponent(b, 2)
             upper_row(b, 2)
             store(b, 2)
-            mirror(b, 2)
             exponent(b, 3)
+            if more_1:
+                q_row_of(b + 1)
+            mirror(b, 2)
             upper_row(b, 3)
             lower_column(b, 2)
             store(b, 3)
-            if more_1:
-                q_row_of(b + 1)

import math
from contextlib import ExitStack

import concourse.mybir as mybir
from concourse.masks import make_identity

F32 = mybir.dt.float32
BF16 = mybir.dt.bfloat16
U32 = mybir.dt.uint32
U8 = mybir.dt.uint8
FP8X4 = mybir.dt.float8_e4m3fn_x4
ACT = mybir.ActivationFunctionType
ALU = mybir.AluOpType

B, F, N = 16, 512, 512
P = 128
PACK = 4
ROWS = N // P
MOMENTUM = 4
MOVING = (512, 512, 256, 128)

HALVES = (slice(0, N // 2), slice(N // 2, N))

FLOPS = 2 * B * N * N * F


def tile_qcdawareold_t_kernel(tc, emb, alpha_p, beta_p, out):
    nc = tc.nc
    with ExitStack() as ctx:
        ctx.enter_context(tc.manual_schedule())
        const = ctx.enter_context(tc.tile_pool(name="const", bufs=1))
        raw_pool = ctx.enter_context(tc.tile_pool(name="raw", bufs=B))
        grouped_pool = ctx.enter_context(tc.tile_pool(name="grouped", bufs=1))
        mx_pool = ctx.enter_context(tc.tile_pool(name="mx", bufs=3))
        stat_pool = ctx.enter_context(tc.tile_pool(name="stat", bufs=4))
        square_pool = ctx.enter_context(tc.tile_pool(name="square", bufs=4))
        diff_pool = ctx.enter_context(tc.tile_pool(name="diff", bufs=4))
        expo_pool = ctx.enter_context(tc.tile_pool(name="expo", bufs=2))
        out_pool = ctx.enter_context(tc.tile_pool(name="outp", bufs=4))
        psum_gram = ctx.enter_context(tc.psum_pool(name="psum_gram", bufs=1))
        psum_q = ctx.enter_context(tc.psum_pool(name="psum_q", bufs=1))
        psum_stage = ctx.enter_context(tc.psum_pool(name="psum_stage", bufs=4))

        mom_rows = const.tile([P, N], BF16)
        nc.vector.memset(mom_rows[:], 0.0)
        nc.sync.dma_start(out=mom_rows[0:B, :], in_=emb[:, MOMENTUM, :])
        alpha_bf = const.tile([P, 1], BF16)
        nc.scalar.dma_start(out=alpha_bf[:], in_=alpha_p.rearrange("a b -> (a b)").partition_broadcast(P))
        beta_bf = const.tile([P, 1], BF16)
        nc.scalar.dma_start(out=beta_bf[:], in_=beta_p.rearrange("a b c -> (a b c)").partition_broadcast(P))

        raw = []
        for b in range(B):
            e_raw = raw_pool.tile([P, PACK, N], BF16)
            features_of_b = emb[b].rearrange("(p t) n -> p t n", t=PACK)
            pieces = HALVES if b == 0 else (slice(0, N),)
            for piece in pieces:
                nc.sync.dma_start(out=e_raw[:, :, piece], in_=features_of_b[:, :, piece])
            raw.append(e_raw)

        ident_bf = const.tile([P, P], BF16)
        make_identity(nc, ident_bf[:])
        ident_f32 = const.tile([P, P], F32)
        make_identity(nc, ident_f32[:])

        two_alpha = const.tile([P, 1], F32)
        nc.vector.tensor_scalar_mul(out=two_alpha[:], in0=alpha_bf[:], scalar1=2.0)
        two_beta_sq = const.tile([P, 1], F32)
        nc.vector.scalar_tensor_tensor(
            out=two_beta_sq[:], in0=beta_bf[:], scalar=2.0, in1=beta_bf[:], op0=ALU.mult, op1=ALU.mult
        )
        mom_cols = psum_stage.tile([P, ROWS, P], BF16, tag="stage")
        for r in range(ROWS):
            nc.tensor.transpose(mom_cols[:, r, :], mom_rows[:, P * r : P * (r + 1)], ident_bf[:])
        log_mom = const.tile([P, ROWS, B], F32)
        nc.scalar.activation(out=log_mom[:], in_=mom_cols[:, :, 0:B], func=ACT.Ln)
        pow_mom = const.tile([P, ROWS, B], F32)
        nc.scalar.activation(out=pow_mom[:], in_=log_mom[:], func=ACT.Exp, scale=two_alpha[:])
        q_col = const.tile([P, ROWS, B], F32)
        nc.gpsimd.tensor_scalar(
            out=q_col[:], in0=pow_mom[:], scalar1=two_beta_sq[:], scalar2=0.0, op0=ALU.mult, op1=ALU.add
        )

        h_cols = {}
        feature_tiles = {}
        square_grams = {}
        h_rows_psum = {}
        h_rows = {}
        q_rows = {}
        grouped_tiles = {}
        code_tiles = {}
        scale_tiles = {}
        gram_homes = {}
        gram_tiles = {}
        flipped_tiles = {}
        diffs = {}
        expo_tiles = {}
        result_tiles = {}

        def features(b, r):
            feat = psum_stage.tile([P, PACK, P], BF16, tag="stage")
            for t in range(PACK):
                nc.tensor.transpose(feat[:, t, :], raw[b][:, t, P * r : P * (r + 1)], ident_bf[:])
            feature_tiles[b, r] = feat

        def sum_squares(b, r):
            squares = square_pool.tile([P, PACK, P], BF16)
            nc.scalar.activation(
                out=squares[:],
                in_=feature_tiles[b, r][:],
                func=ACT.Square,
                scale=math.sqrt(0.5),
                accum_out=h_cols[b][:, r : r + 1],
            )

        def open_norms(b):
            h_cols[b] = stat_pool.tile([P, ROWS], F32, name="h_col")

        def square_gram(b, r):
            gram = psum_stage.tile([P, P], F32, tag="stage")
            for t in range(PACK):
                block = raw[b][:, t, P * r : P * (r + 1)]
                nc.tensor.matmul(gram[:], lhsT=block, rhs=block, start=(t == 0), stop=(t == PACK - 1))
            square_grams[b, r] = gram

        def sum_diagonal(b, r):
            diagonal = square_pool.tile([P, P], F32)
            nc.vector.scalar_tensor_tensor(
                out=diagonal[:],
                in0=square_grams[b, r][:],
                scalar=0.5,
                in1=ident_f32[:],
                op0=ALU.mult,
                op1=ALU.mult,
                accum_out=h_cols[b][:, r : r + 1],
            )

        def spread(row, column_of):
            for r in range(ROWS):
                nc.tensor.transpose(row[:, P * r : P * (r + 1)], column_of(r).to_broadcast([P, P]), ident_f32[:])

        def spread_h(b):
            h_col = h_cols[b]
            h_row_psum = psum_stage.tile([P, N], F32, tag="stage")
            spread(h_row_psum, lambda r: h_col[:, r : r + 1])
            h_rows_psum[b] = h_row_psum

        def h_row_to_sbuf(b):
            h_row = stat_pool.tile([P, N], F32)
            nc.vector.tensor_copy(out=h_row[:], in_=h_rows_psum[b][:])
            h_rows[b] = h_row

        def q_row_of(b):
            q_row = psum_q.tile([P, N], F32)
            spread(q_row, lambda r: q_col[:, r, b : b + 1])
            q_rows[b] = q_row

        def regroup(b):
            grouped = grouped_pool.tile([P, N, PACK], BF16, align_bytes=64)
            nc.gpsimd.tensor_scalar(
                out=grouped[:],
                in0=raw[b][:].rearrange("p t n -> p n t"),
                scalar1=1.0,
                scalar2=0.0,
                op0=ALU.mult,
                op1=ALU.add,
            )
            grouped_tiles[b] = grouped

        def quantise(b):
            codes = mx_pool.tile([P, N], U32, align_bytes=64)
            scales = mx_pool.tile([P, N], U8, align_bytes=64)
            nc.vector.quantize_mx(
                out=codes[:].bitcast(FP8X4),
                scales=scales[:],
                in_=grouped_tiles[b][:].rearrange("p n t -> p (n t)"),
            )
            code_tiles[b] = codes
            scale_tiles[b] = scales

        def open_gram(b):
            gram_0 = psum_gram.tile([P, N], F32)
            gram_1 = psum_gram.tile([P, N], F32)
            gram_23 = psum_gram.tile([P, N], F32)
            gram_homes[b] = (gram_0[:, 0:N], gram_1[:, 0:N], gram_23[:, 2 * P : N], gram_23[:, 0:P])
            gram_tiles[b] = (gram_0[:, 0:N], gram_1[:, P:N], gram_23[:, 2 * P : N], gram_23[:, 0:P])

        def gram_rows(b, rows):
            codes, scales = code_tiles[b], scale_tiles[b]
            for r in rows:
                first = N - MOVING[r]
                nc.tensor.matmul_mx(
                    out=gram_homes[b][r],
                    lhsT=codes[:, P * r : P * (r + 1)].bitcast(FP8X4),
                    lhsT_scale=scales[:, P * r : P * (r + 1)],
                    rhs=codes[:, first:N].bitcast(FP8X4),
                    rhs_scale=scales[:, first:N],
                    start=True,
                    stop=True,
                )

        def store(b, r):
            nc.sync.dma_start(out=out[b, P * r : P * (r + 1), :], in_=result_tiles[b][:, r, :])

        def open_batch(b):
            expo_tiles[b] = expo_pool.tile([P, ROWS, N], F32, name="expo")
            result_tiles[b] = out_pool.tile([P, ROWS, N], F32, name="result")

        def difference(b, r):
            diff = diff_pool.tile([P, N], F32)
            nc.vector.scalar_tensor_tensor(
                out=diff[:, P * r : N],
                in0=gram_tiles[b][r],
                scalar=h_cols[b][:, r : r + 1],
                in1=h_rows[b][:, P * r : N],
                op0=ALU.subtract,
                op1=ALU.subtract,
            )
            diffs[r] = diff

        def exponent(b, r):
            nc.vector.scalar_tensor_tensor(
                out=expo_tiles[b][:, r, P * r : N],
                in0=q_rows[b][:, P * r : N],
                scalar=q_col[:, r, b : b + 1],
                in1=diffs[r][:, P * r : N],
                op0=ALU.min,
                op1=ALU.mult,
            )

        def upper_row(b, r):
            nc.scalar.activation(
                out=result_tiles[b][:, r, P * r : N], in_=expo_tiles[b][:, r, P * r : N], func=ACT.Exp
            )

        def mirror(b, c):
            below = ROWS - 1 - c
            flipped = psum_stage.tile([P, below, P], F32, tag="stage")
            for k in range(below):
                r = c + 1 + k
                nc.tensor.transpose(flipped[:, k, :], expo_tiles[b][:, c, P * r : P * (r + 1)], ident_f32[:])
            flipped_tiles[b, c] = flipped

        def lower_column(b, c):
            nc.scalar.activation(
                out=result_tiles[b][:, c + 1 : ROWS, P * c : P * (c + 1)], in_=flipped_tiles[b, c][:], func=ACT.Exp
            )

        first_grouped = grouped_pool.tile([P, N, PACK], BF16, align_bytes=64, name="grouped")
        for half in HALVES:
            nc.vector.tensor_copy(out=first_grouped[:, half, :], in_=raw[0][:, :, half].rearrange("p t n -> p n t"))
        grouped_tiles[0] = first_grouped
        open_norms(0)
        quantise(0)
        features(0, 0)
        sum_squares(0, 0)
        for r in (1, 2, 3):
            square_gram(0, r)
            sum_diagonal(0, r)
        spread_h(0)
        h_row_to_sbuf(0)
        regroup(1)
        open_gram(0)
        gram_rows(0, (0, 1, 2, 3))
        q_row_of(0)
        open_norms(1)
        for r in (0, 1):
            features(1, r)
            sum_squares(1, r)
        for r in (2, 3):
            square_gram(1, r)
        for b in range(B):
            more_1 = b + 1 < B
            more_2 = b + 2 < B
            open_batch(b)
            difference(b, 0)
            difference(b, 1)
            exponent(b, 0)
            if more_2:
                open_norms(b + 2)
                square_gram(b + 2, ROWS - 1)
                features(b + 2, 0)
                sum_squares(b + 2, 0)
            upper_row(b, 0)
            store(b, 0)
            mirror(b, 0)
            lower_column(b, 0)
            difference(b, 2)
            if b == 0:
                for r in (2, 3):
                    sum_diagonal(1, r)
            if more_1:
                quantise(b + 1)
                spread_h(b + 1)
            if more_2:
                regroup(b + 2)
                sum_diagonal(b + 2, ROWS - 1)
                features(b + 2, 1)
                sum_squares(b + 2, 1)
            exponent(b, 1)
            if more_1:
                open_gram(b + 1)
            upper_row(b, 1)
            mirror(b, 1)
            lower_column(b, 1)
            store(b, 1)
            difference(b, 3)
            if more_1:
                h_row_to_sbuf(b + 1)
                gram_rows(b + 1, (0, 1, 2, 3))
            if more_2:
                features(b + 2, 2)
                sum_squares(b + 2, 2)
            exponent(b, 2)
            upper_row(b, 2)
            store(b, 2)
            exponent(b, 3)
            if more_1:
                q_row_of(b + 1)
            mirror(b, 2)
            upper_row(b, 3)
            lower_column(b, 2)
            store(b, 3)
